import numpy as np
import ml_dtypes


def mxq(x, axis, fmt="e4m3"):
    dtype, down = {"e4m3": (ml_dtypes.float8_e4m3fn, 7), "e5m2": (ml_dtypes.float8_e5m2, 14)}[fmt]
    v = np.moveaxis(np.asarray(x, np.float32).astype(ml_dtypes.bfloat16).astype(np.float64), axis, -1)
    blocks = v.reshape(v.shape[:-1] + (-1, 32))
    amax = np.abs(blocks).max(-1, keepdims=True)
    byte = np.maximum(np.where(amax > 0, np.frexp(amax)[1] - 1 + 127, 0) - down, 1)
    scale = np.exp2(byte - 127.0)
    codes = (blocks / scale).astype(np.float32).astype(dtype).astype(np.float64)
    return np.moveaxis((codes * scale).reshape(v.shape), -1, axis)


WIDE = False


def mx_kscale(k):
    if not WIDE:
        return np.ones(k)
    levels = np.array([10, -10, 5, -5, 0])
    a = np.random.permutation(np.resize(levels, k // 512 * 4)).reshape(k // 512, 4)
    idx = np.arange(k)
    return np.exp2(a[idx // 512, idx % 128 // 32])


BF16 = ml_dtypes.bfloat16


def bf(x):
    return np.asarray(x, np.float32).astype(BF16)


def f64(x):
    return np.asarray(x).astype(np.float64)


B, S, P, F, O, DEG, R = 8, 512, 2, 512, 128, 16, 4
OC = O + O + O


def rows(scale):
    return np.random.standard_normal((B, S, P, F)) * np.exp(0.4 * np.random.standard_normal((B, S, P, 1))) * scale


def setup_inputs():
    s = mx_kscale(F)
    return {"x": bf(rows(1.0) * s), "nb": bf(rows(1.0 / np.sqrt(DEG)) * s), "mu": bf(rows(1.0) * s),
            "Wx_w": bf(np.random.standard_normal((O, F)) / np.sqrt(F) / s), "Wx_b": bf(0.1 * np.random.standard_normal(O)),
            "Wn_w": bf(np.random.standard_normal((O, F)) / np.sqrt(F) / s), "Wn_b": bf(0.1 * np.random.standard_normal(O)),
            "Wr_w": bf(np.random.standard_normal((O, F)) / np.sqrt(F) / s), "Wr_b": bf(0.1 * np.random.standard_normal(O)),
            "bn_gamma": bf(1.0 + 0.1 * np.random.standard_normal(OC)), "bn_beta": bf(0.1 * np.random.standard_normal(OC))}


def lin(x, w, b):
    return (mxq(x, 3, "e4m3") @ mxq(w, 1, "e4m3").T) + b


def reference(x, nb, mu, Wx_w, Wx_b, Wn_w, Wn_b, Wr_w, Wr_b, bn_gamma, bn_beta):
    h = np.concatenate([lin(f64(x), f64(Wx_w), f64(Wx_b)), lin(f64(nb), f64(Wn_w), f64(Wn_b)), lin(f64(mu), f64(Wr_w), f64(Wr_b))], axis=-1)
    n = np.maximum(np.sqrt((h ** 2).sum(3, keepdims=True)), 1e-12)
    r = np.maximum(h / n, 0.0)
    m = r.mean(axis=(0, 1, 2))
    v = r.var(axis=(0, 1, 2))
    return (r - m) / np.sqrt(v + 1e-5) * f64(bn_gamma) + f64(bn_beta)

@@ -1,0 +1,340 @@
+from contextlib import ExitStack
+
+import concourse.mybir as mybir
+from concourse.masks import make_identity
+
+F32 = mybir.dt.float32
+BF16 = mybir.dt.bfloat16
+U8 = mybir.dt.uint8
+U32 = mybir.dt.uint32
+FP8X4 = mybir.dt.float8_e4m3fn_x4
+ALU = mybir.AluOpType
+ACT = mybir.ActivationFunctionType
+
+P = 128
+ROWS = 8192
+K = 512
+NS = 3
+OC = NS * P
+NT = ROWS // P
+TG = 4
+NR = NT // TG
+FLOPS = 2 * ROWS * K * OC
+
+PIN = True
+XS_BUFS = 3
+V_EVAC = ()
+S_P3 = (3,)
+S_GROUPS = (0, 2, 4, 6, 8, 10, 12, 14)
+
+
+def tile_batchedgraphsagemean1_pb_t_kernel(
+    tc, x, nb, mu, Wx_w, Wx_b, Wn_w, Wn_b, Wr_w, Wr_b, bn_gamma, bn_beta, out
+):
+    nc = tc.nc
+    feats = [a.flatten_outer_dims().rearrange("(p t) k -> p t k", t=NT) for a in (x, nb, mu)]
+    out_v = out.flatten_outer_dims().rearrange("(p t) c -> p t c", t=NT)
+    weights = (Wx_w, Wn_w, Wr_w)
+    biases = (Wx_b, Wn_b, Wr_b)
+
+    with ExitStack() as ctx:
+        if PIN:
+            ctx.enter_context(tc.manual_schedule())
+        const = ctx.enter_context(tc.tile_pool(name="const", bufs=1))
+        loads = ctx.enter_context(tc.tile_pool(name="loads", bufs=XS_BUFS))
+        work = ctx.enter_context(tc.tile_pool(name="work", bufs=2))
+        psum = ctx.enter_context(tc.psum_pool(name="psum", bufs=8))
+
+        res = const.tile([P, NT, OC], F32, name="res")
+        ident = const.tile([P, P], F32, name="ident")
+        small_bf = const.tile([P, P], BF16, name="small_bf")
+        small_f = const.tile([P, P], F32, name="small_f")
+        cols = const.tile([P, 9], F32, name="cols")
+        bias_b = const.tile([P, OC], F32, name="bias_b")
+        w_sb = const.tile([P, NS, K], BF16, name="w_sb")
+        w_grp = const.tile([P, NS * K], BF16, name="w_grp", align_bytes=64)
+        w_codes = const.tile([P, NS * P], U32, name="w_codes", align_bytes=64)
+        w_scl = const.tile([P, NS * P], U8, name="w_scl", align_bytes=64)
+        n2 = const.tile([P, NT], F32, name="n2")
+        nrm = const.tile([P, NT], F32, name="nrm")
+        nrmc = const.tile([P, NT], F32, name="nrmc")
+        invn = const.tile([P, NT], F32, name="invn")
+        stats = const.tile([P, NS, NR, 6], F32, name="stats")
+        mv = const.tile([P, NS, 2], F32, name="mv")
+        veps = const.tile([P, NS], F32, name="veps")
+        sdev = const.tile([P, NS], F32, name="sdev")
+        rstd = const.tile([P, NS], F32, name="rstd")
+        gain = const.tile([P, NS], F32, name="gain")
+        mgain = const.tile([P, NS], F32, name="mgain")
+        shift = const.tile([P, NS], F32, name="shift")
+
+        xs = {}
+        grp = {}
+        codes = {}
+        scl = {}
+        mxb = {}
+        fbk = {}
+
+        def new_bank(label):
+            bank = psum.tile([P, 512], F32, name=label, tag="bank")
+            return bank
+
+        def word_transposes(bank, a, src_bf):
+            src = src_bf.bitcast(F32)
+            for u in range(2):
+                c = (2 * a + u) * P
+                nc.tensor.transpose(out=bank[:, c : c + P], in_=src[:, u * P : (u + 1) * P], identity=ident[:])
+
+        def load(g):
+            for s in range(NS):
+                t = loads.tile([P, TG, K], BF16, name="xs%d" % s, tag="xs%d" % s)
+                xs[(g, s)] = t
+                nc.sync.dma_start(out=t[:], in_=feats[s][:, g * TG : (g + 1) * TG, :])
+
+        def t_in(g):
+            for s in range(NS):
+                gt = work.tile([P, TG * K], BF16, name="grp%d" % s, tag="grp%d" % s, align_bytes=64)
+                grp[(g, s)] = gt
+                g32 = gt[:].bitcast(F32)
+                for h in range(TG // 2):
+                    bank = new_bank("xt")
+                    for a in range(2):
+                        word_transposes(bank, a, xs[(g, s)][:, 2 * h + a, :])
+                    dst = g32[:, h * 512 : (h + 1) * 512].rearrange("p (a r u) -> p a r u", a=2, u=2)
+                    src = bank[:].rearrange("p (a u r) -> p a r u", a=2, u=2)
+                    if (s * 2 + h) in V_EVAC:
+                        nc.vector.tensor_copy(out=dst, in_=src)
+                    else:
+                        nc.scalar.copy(out=dst, in_=src)
+
+        def quant(g):
+            for s in range(NS):
+                ct = work.tile([P, TG * P], U32, name="codes%d" % s, tag="codes%d" % s, align_bytes=64)
+                st = work.tile([P, TG * P], U8, name="scl%d" % s, tag="scl%d" % s, align_bytes=64)
+                codes[(g, s)] = ct
+                scl[(g, s)] = st
+                nc.vector.quantize_mx(out=ct[:].bitcast(FP8X4), scales=st[:], in_=grp[(g, s)][:])
+
+        def mx(g):
+            for s in range(NS):
+                bank = new_bank("mx")
+                mxb[(g, s)] = bank
+                for j in range(TG):
+                    nc.tensor.matmul_mx(
+                        out=bank[:, j * P : (j + 1) * P],
+                        lhsT=codes[(g, s)][:, j * P : (j + 1) * P].bitcast(FP8X4),
+                        lhsT_scale=scl[(g, s)][:, j * P : (j + 1) * P],
+                        rhs=w_codes[:, s * P : (s + 1) * P].bitcast(FP8X4),
+                        rhs_scale=w_scl[:, s * P : (s + 1) * P],
+                        start=True,
+                        stop=True,
+                    )
+
+        def p1(g):
+            for s in range(NS):
+                nc.vector.tensor_tensor(
+                    out=res[:, g * TG : (g + 1) * TG, s * P : (s + 1) * P],
+                    in0=mxb[(g, s)][:].rearrange("p (j c) -> p j c", j=TG),
+                    in1=bias_b[:, s * P : (s + 1) * P].unsqueeze(1).to_broadcast([P, TG, P]),
+                    op=ALU.add,
+                )
+
+        def p2(g):
+            for j in range(TG):
+                t = g * TG + j
+                junk = work.tile([P, OC], F32, name="junk", tag="junk")
+                nc.scalar.activation(out=junk[:], in_=res[:, t, :], func=ACT.Square, accum_out=n2[:, t : t + 1])
+            nc.scalar.sqrt(out=nrm[:, g * TG : (g + 1) * TG], in_=n2[:, g * TG : (g + 1) * TG])
+
+        def norm(g):
+            sl = slice(g * TG, (g + 1) * TG)
+            nc.vector.tensor_scalar_max(out=nrmc[:, sl], in0=nrm[:, sl], scalar1=1e-12)
+            nc.vector.reciprocal(out=invn[:, sl], in_=nrmc[:, sl])
+
+        def p3(g):
+            for j in range(TG):
+                t = g * TG + j
+                if j in S_P3:
+                    nc.scalar.activation(out=res[:, t, :], in_=res[:, t, :], func=ACT.Relu, scale=invn[:, t : t + 1])
+                else:
+                    nc.vector.tensor_scalar(
+                        out=res[:, t, :],
+                        in0=res[:, t, :],
+                        scalar1=invn[:, t : t + 1],
+                        scalar2=0.0,
+                        op0=ALU.mult,
+                        op1=ALU.max,
+                    )
+
+        def flip(g, label):
+            for s in range(NS):
+                bank = new_bank(label)
+                fbk[(g, s)] = bank
+                for j in range(TG):
+                    nc.tensor.transpose(
+                        out=bank[:, j * P : (j + 1) * P],
+                        in_=res[:, g * TG + j, s * P : (s + 1) * P],
+                        identity=ident[:],
+                    )
+
+        def bn(g):
+            for s in range(NS):
+                nc.vector.bn_stats(out=stats[:, s, g, :], in_=fbk[(g, s)][:])
+
+        def spread(bank, vec, m):
+            nc.tensor.matmul(
+                out=bank[:, m * P : (m + 1) * P],
+                lhsT=vec.to_broadcast([P, P]),
+                rhs=ident[:],
+                start=True,
+                stop=True,
+            )
+
+        nc.vector.memset(small_bf[:], 0.0)
+        make_identity(nc, ident[:])
+        load(0)
+        for s in range(NS):
+            nc.scalar.dma_start(out=w_sb[:, s, :], in_=weights[s])
+        for s in range(NS):
+            nc.scalar.dma_start(out=small_bf[s : s + 1, :], in_=biases[s].unsqueeze(0))
+        nc.scalar.dma_start(out=small_bf[3:6, :], in_=bn_gamma.rearrange("(s c) -> s c", s=NS))
+        nc.scalar.dma_start(out=small_bf[6:9, :], in_=bn_beta.rearrange("(s c) -> s c", s=NS))
+        load(1)
+
+        wb0 = new_bank("wb0")
+        word_transposes(wb0, 0, w_sb[:, 0, :])
+        word_transposes(wb0, 1, w_sb[:, 1, :])
+        wb1 = new_bank("wb1")
+        word_transposes(wb1, 0, w_sb[:, 2, :])
+        wg32 = w_grp[:].bitcast(F32)
+        nc.vector.tensor_copy(
+            out=wg32[:, 0:512].rearrange("p (a r u) -> p a r u", a=2, u=2),
+            in_=wb0[:].rearrange("p (a u r) -> p a r u", a=2, u=2),
+        )
+        nc.vector.tensor_copy(
+            out=wg32[:, 512:768].rearrange("p (r u) -> p r u", u=2),
+            in_=wb1[:, 0:256].rearrange("p (u r) -> p r u", u=2),
+        )
+
+        def setup_small():
+            for s in range(NS):
+                nc.vector.quantize_mx(
+                    out=w_codes[:, s * P : (s + 1) * P].bitcast(FP8X4),
+                    scales=w_scl[:, s * P : (s + 1) * P],
+                    in_=w_grp[:, s * K : (s + 1) * K],
+                )
+            nc.vector.tensor_copy(out=small_f[:], in_=small_bf[:])
+            sb = new_bank("sb")
+            nc.tensor.transpose(out=sb[:, 0:P], in_=small_f[:], identity=ident[:])
+            nc.vector.tensor_copy(out=cols[:], in_=sb[:, 0:9])
+            bb = new_bank("bb")
+            for s in range(NS):
+                spread(bb, cols[:, s : s + 1], s)
+            nc.vector.tensor_copy(out=bias_b[:], in_=bb[:, 0:OC])
+
+        for k in range(NR + 3):
+            if k + 2 < NR:
+                load(k + 2)
+            if 0 <= k - 2 < NR:
+                p2(k - 2)
+            if 0 <= k - 3 < NR:
+                flip(k - 3, "fl")
+            if k < NR:
+                t_in(k)
+            if k == 0:
+                setup_small()
+            if 0 <= k - 1 < NR:
+                quant(k - 1)
+            if 0 <= k - 3 < NR:
+                bn(k - 3)
+            if 0 <= k - 1 < NR:
+                mx(k - 1)
+                p1(k - 1)
+            if 0 <= k - 2 < NR:
+                norm(k - 2)
+                p3(k - 2)
+
+        s_groups = list(S_GROUPS)
+        v_groups = [g for g in range(NR) if g not in S_GROUPS]
+        flip(s_groups[0], "f1")
+        for s in range(NS):
+            nc.vector.bn_aggr(out=mv[:, s, :], in_=stats[:, s, :, :].rearrange("p g x -> p (g x)"))
+        nc.vector.tensor_scalar_add(out=veps[:], in0=mv[:, :, 1], scalar1=1e-5)
+        nc.scalar.sqrt(out=sdev[:], in_=veps[:])
+        nc.vector.reciprocal(out=rstd[:], in_=sdev[:])
+        nc.vector.tensor_mul(out=gain[:], in0=cols[:, 3:6], in1=rstd[:])
+        nc.vector.tensor_mul(out=mgain[:], in0=mv[:, :, 0], in1=gain[:])
+        nc.vector.tensor_sub(out=shift[:], in0=cols[:, 6:9], in1=mgain[:])
+        a_bank = new_bank("a_bank")
+        b_bank = new_bank("b_bank")
+        for s in range(NS):
+            spread(a_bank, gain[:, s : s + 1], s)
+        for s in range(NS):
+            spread(b_bank, shift[:, s : s + 1], s)
+
+        o_t = {}
+        obk = {}
+
+        def affine(g):
+            for s in range(NS):
+                ot = work.tile([P, TG * P], F32, name="ot%d" % s, tag="ot%d" % s)
+                o_t[(g, s)] = ot
+                nc.scalar.activation(
+                    out=ot[:],
+                    in_=fbk[(g, s)][:],
+                    func=ACT.Identity,
+                    scale=gain[:, s : s + 1],
+                    bias=shift[:, s : s + 1],
+                )
+
+        def flip_back(g):
+            for s in range(NS):
+                bank = new_bank("f2")
+                obk[(g, s)] = bank
+                for j in range(TG):
+                    nc.tensor.transpose(
+                        out=bank[:, j * P : (j + 1) * P],
+                        in_=o_t[(g, s)][:, j * P : (j + 1) * P],
+                        identity=ident[:],
+                    )
+
+        def copy_back(g):
+            for s in range(NS):
+                nc.scalar.copy(
+                    out=res[:, g * TG : (g + 1) * TG, s * P : (s + 1) * P],
+                    in_=obk[(g, s)][:].rearrange("p (j c) -> p j c", j=TG),
+                )
+
+        def store(g):
+            nc.sync.dma_start(out=out_v[:, g * TG : (g + 1) * TG, :], in_=res[:, g * TG : (g + 1) * TG, :])
+
+        def v_scale(g, bank, op):
+            rs = res[:, g * TG : (g + 1) * TG, :]
+            nc.vector.tensor_tensor(
+                out=rs, in0=rs, in1=bank[:, 0:OC].unsqueeze(1).to_broadcast([P, TG, OC]), op=op
+            )
+
+        n_s = len(s_groups)
+        n_v = len(v_groups)
+
+        def v_pair(first):
+            pair = v_groups[first : first + 2]
+            for g in pair:
+                v_scale(g, a_bank, ALU.mult)
+            for g in pair:
+                v_scale(g, b_bank, ALU.add)
+                store(g)
+
+        affine(s_groups[0])
+        for i in range(n_s):
+            if i + 1 < n_s:
+                flip(s_groups[i + 1], "f1")
+            flip_back(s_groups[i])
+            if i % 2 == 0 and i < n_v:
+                v_pair(i)
+            if i + 1 < n_s:
+                affine(s_groups[i + 1])
+            copy_back(s_groups[i])
+            store(s_groups[i])
+        for i in range((n_s + 1) // 2 * 2, n_v, 2):
+            v_pair(i)

@@ -23,8 +23,9 @@ FLOPS = 2 * ROWS * K * OC
 
 PIN = True
 XS_BUFS = 3
-V_EVAC = ()
-S_P3 = (3,)
+V_EVAC_ROUNDS = 1
+DUMMY = True
+TAIL_WARM = True
 S_GROUPS = (0, 2, 4, 6, 8, 10, 12, 14)
 
 
@@ -43,6 +44,7 @@ def tile_batchedgraphsagemean1_pb_t_kernel(
         const = ctx.enter_context(tc.tile_pool(name="const", bufs=1))
         loads = ctx.enter_context(tc.tile_pool(name="loads", bufs=XS_BUFS))
         work = ctx.enter_context(tc.tile_pool(name="work", bufs=2))
+        tailp = ctx.enter_context(tc.tile_pool(name="tailp", bufs=3))
         psum = ctx.enter_context(tc.psum_pool(name="psum", bufs=8))
 
         res = const.tile([P, NT, OC], F32, name="res")
@@ -85,65 +87,78 @@ def tile_batchedgraphsagemean1_pb_t_kernel(
                 c = (2 * a + u) * P
                 nc.tensor.transpose(out=bank[:, c : c + P], in_=src[:, u * P : (u + 1) * P], identity=ident[:])
 
-        def load(g):
-            for s in range(NS):
-                t = loads.tile([P, TG, K], BF16, name="xs%d" % s, tag="xs%d" % s)
-                xs[(g, s)] = t
-                nc.sync.dma_start(out=t[:], in_=feats[s][:, g * TG : (g + 1) * TG, :])
-
-        def t_in(g):
-            for s in range(NS):
-                gt = work.tile([P, TG * K], BF16, name="grp%d" % s, tag="grp%d" % s, align_bytes=64)
-                grp[(g, s)] = gt
-                g32 = gt[:].bitcast(F32)
-                for h in range(TG // 2):
-                    bank = new_bank("xt")
-                    for a in range(2):
-                        word_transposes(bank, a, xs[(g, s)][:, 2 * h + a, :])
-                    dst = g32[:, h * 512 : (h + 1) * 512].rearrange("p (a r u) -> p a r u", a=2, u=2)
-                    src = bank[:].rearrange("p (a u r) -> p a r u", a=2, u=2)
-                    if (s * 2 + h) in V_EVAC:
-                        nc.vector.tensor_copy(out=dst, in_=src)
-                    else:
-                        nc.scalar.copy(out=dst, in_=src)
-
-        def quant(g):
-            for s in range(NS):
-                ct = work.tile([P, TG * P], U32, name="codes%d" % s, tag="codes%d" % s, align_bytes=64)
-                st = work.tile([P, TG * P], U8, name="scl%d" % s, tag="scl%d" % s, align_bytes=64)
-                codes[(g, s)] = ct
-                scl[(g, s)] = st
-                nc.vector.quantize_mx(out=ct[:].bitcast(FP8X4), scales=st[:], in_=grp[(g, s)][:])
-
-        def mx(g):
-            for s in range(NS):
-                bank = new_bank("mx")
-                mxb[(g, s)] = bank
-                for j in range(TG):
-                    nc.tensor.matmul_mx(
-                        out=bank[:, j * P : (j + 1) * P],
-                        lhsT=codes[(g, s)][:, j * P : (j + 1) * P].bitcast(FP8X4),
-                        lhsT_scale=scl[(g, s)][:, j * P : (j + 1) * P],
-                        rhs=w_codes[:, s * P : (s + 1) * P].bitcast(FP8X4),
-                        rhs_scale=w_scl[:, s * P : (s + 1) * P],
-                        start=True,
-                        stop=True,
-                    )
-
-        def p1(g):
-            for s in range(NS):
-                nc.vector.tensor_tensor(
-                    out=res[:, g * TG : (g + 1) * TG, s * P : (s + 1) * P],
-                    in0=mxb[(g, s)][:].rearrange("p (j c) -> p j c", j=TG),
-                    in1=bias_b[:, s * P : (s + 1) * P].unsqueeze(1).to_broadcast([P, TG, P]),
-                    op=ALU.add,
+        def load(g, s, parts):
+            t = loads.tile([P, TG, K], BF16, name="xs%d" % s, tag="xs%d" % s)
+            xs[(g, s)] = t
+            w = TG // parts
+            for i in range(parts):
+                nc.sync.dma_start(
+                    out=t[:, i * w : (i + 1) * w, :], in_=feats[s][:, g * TG + i * w : g * TG + (i + 1) * w, :]
                 )
 
-        def p2(g):
+        def t_in(g, s):
+            gt = work.tile([P, TG * K], BF16, name="grp%d" % s, tag="grp%d" % s, align_bytes=64)
+            grp[(g, s)] = gt
+            g32 = gt[:].bitcast(F32)
+            for h in range(TG // 2):
+                bank = new_bank("xt")
+                for a in range(2):
+                    word_transposes(bank, a, xs[(g, s)][:, 2 * h + a, :])
+                dst = g32[:, h * 512 : (h + 1) * 512].rearrange("p (a r u) -> p a r u", a=2, u=2)
+                src = bank[:].rearrange("p (a u r) -> p a r u", a=2, u=2)
+                if g < V_EVAC_ROUNDS and h == 1:
+                    nc.vector.tensor_copy(out=dst, in_=src)
+                else:
+                    nc.scalar.copy(out=dst, in_=src)
+
+        def quant(g, s):
+            ct = work.tile([P, TG * P], U32, name="codes%d" % s, tag="codes%d" % s, align_bytes=64)
+            st = work.tile([P, TG * P], U8, name="scl%d" % s, tag="scl%d" % s, align_bytes=64)
+            codes[(g, s)] = ct
+            scl[(g, s)] = st
+            nc.vector.quantize_mx(out=ct[:].bitcast(FP8X4), scales=st[:], in_=grp[(g, s)][:])
+
+        def clock_pass(bank, key):
+            nc.tensor.matmul_mx(
+                out=bank[:],
+                lhsT=codes[key][:, 0:P].bitcast(FP8X4),
+                lhsT_scale=scl[key][:, 0:P],
+                rhs=codes[key][:].bitcast(FP8X4),
+                rhs_scale=scl[key][:],
+                start=True,
+                stop=True,
+            )
+
+        def mx(g, s):
+            bank = new_bank("mx")
+            mxb[(g, s)] = bank
+            if DUMMY:
+                clock_pass(bank, (g, s))
             for j in range(TG):
-                t = g * TG + j
-                junk = work.tile([P, OC], F32, name="junk", tag="junk")
-                nc.scalar.activation(out=junk[:], in_=res[:, t, :], func=ACT.Square, accum_out=n2[:, t : t + 1])
+                nc.tensor.matmul_mx(
+                    out=bank[:, j * P : (j + 1) * P],
+                    lhsT=codes[(g, s)][:, j * P : (j + 1) * P].bitcast(FP8X4),
+                    lhsT_scale=scl[(g, s)][:, j * P : (j + 1) * P],
+                    rhs=w_codes[:, s * P : (s + 1) * P].bitcast(FP8X4),
+                    rhs_scale=w_scl[:, s * P : (s + 1) * P],
+                    start=True,
+                    stop=True,
+                )
+
+        def p1(g, s):
+            nc.vector.tensor_tensor(
+                out=res[:, g * TG : (g + 1) * TG, s * P : (s + 1) * P],
+                in0=mxb[(g, s)][:].rearrange("p (j c) -> p j c", j=TG),
+                in1=bias_b[:, s * P : (s + 1) * P].unsqueeze(1).to_broadcast([P, TG, P]),
+                op=ALU.add,
+            )
+
+        def p2(g, j):
+            t = g * TG + j
+            junk = work.tile([P, OC], F32, name="junk", tag="junk")
+            nc.scalar.activation(out=junk[:], in_=res[:, t, :], func=ACT.Square, accum_out=n2[:, t : t + 1])
+
+        def root(g):
             nc.scalar.sqrt(out=nrm[:, g * TG : (g + 1) * TG], in_=n2[:, g * TG : (g + 1) * TG])
 
         def norm(g):
@@ -151,35 +166,34 @@ def tile_batchedgraphsagemean1_pb_t_kernel(
             nc.vector.tensor_scalar_max(out=nrmc[:, sl], in0=nrm[:, sl], scalar1=1e-12)
             nc.vector.reciprocal(out=invn[:, sl], in_=nrmc[:, sl])
 
-        def p3(g):
+        def p3(g, j, on_scalar):
+            t = g * TG + j
+            if on_scalar:
+                nc.scalar.activation(out=res[:, t, :], in_=res[:, t, :], func=ACT.Relu, scale=invn[:, t : t + 1])
+            else:
+                nc.vector.tensor_scalar(
+                    out=res[:, t, :],
+                    in0=res[:, t, :],
+                    scalar1=invn[:, t : t + 1],
+                    scalar2=0.0,
+                    op0=ALU.mult,
+                    op1=ALU.max,
+                )
+
+        def flip(g, s, label, warm):
+            bank = new_bank(label)
+            fbk[(g, s)] = bank
+            if warm:
+                clock_pass(bank, (NR - 1, NS - 1))
             for j in range(TG):
-                t = g * TG + j
-                if j in S_P3:
-                    nc.scalar.activation(out=res[:, t, :], in_=res[:, t, :], func=ACT.Relu, scale=invn[:, t : t + 1])
-                else:
-                    nc.vector.tensor_scalar(
-                        out=res[:, t, :],
-                        in0=res[:, t, :],
-                        scalar1=invn[:, t : t + 1],
-                        scalar2=0.0,
-                        op0=ALU.mult,
-                        op1=ALU.max,
-                    )
+                nc.tensor.transpose(
+                    out=bank[:, j * P : (j + 1) * P],
+                    in_=res[:, g * TG + j, s * P : (s + 1) * P],
+                    identity=ident[:],
+                )
 
-        def flip(g, label):
-            for s in range(NS):
-                bank = new_bank(label)
-                fbk[(g, s)] = bank
-                for j in range(TG):
-                    nc.tensor.transpose(
-                        out=bank[:, j * P : (j + 1) * P],
-                        in_=res[:, g * TG + j, s * P : (s + 1) * P],
-                        identity=ident[:],
-                    )
-
-        def bn(g):
-            for s in range(NS):
-                nc.vector.bn_stats(out=stats[:, s, g, :], in_=fbk[(g, s)][:])
+        def bn(g, s):
+            nc.vector.bn_stats(out=stats[:, s, g, :], in_=fbk[(g, s)][:])
 
         def spread(bank, vec, m):
             nc.tensor.matmul(
@@ -190,73 +204,106 @@ def tile_batchedgraphsagemean1_pb_t_kernel(
                 stop=True,
             )
 
+        def valid(n):
+            g, s = divmod(n, NS)
+            return (g, s) if 0 <= n and g < NR else None
+
         nc.vector.memset(small_bf[:], 0.0)
         make_identity(nc, ident[:])
-        load(0)
+        load(0, 0, 2)
         for s in range(NS):
-            nc.scalar.dma_start(out=w_sb[:, s, :], in_=weights[s])
+            nc.sync.dma_start(out=w_sb[:, s, :], in_=weights[s])
         for s in range(NS):
             nc.scalar.dma_start(out=small_bf[s : s + 1, :], in_=biases[s].unsqueeze(0))
         nc.scalar.dma_start(out=small_bf[3:6, :], in_=bn_gamma.rearrange("(s c) -> s c", s=NS))
         nc.scalar.dma_start(out=small_bf[6:9, :], in_=bn_beta.rearrange("(s c) -> s c", s=NS))
-        load(1)
+        load(0, 1, 1)
+        load(0, 2, 1)
+        for s in range(NS):
+            load(1, s, 1)
 
-        wb0 = new_bank("wb0")
-        word_transposes(wb0, 0, w_sb[:, 0, :])
-        word_transposes(wb0, 1, w_sb[:, 1, :])
-        wb1 = new_bank("wb1")
-        word_transposes(wb1, 0, w_sb[:, 2, :])
-        wg32 = w_grp[:].bitcast(F32)
-        nc.vector.tensor_copy(
-            out=wg32[:, 0:512].rearrange("p (a r u) -> p a r u", a=2, u=2),
-            in_=wb0[:].rearrange("p (a u r) -> p a r u", a=2, u=2),
-        )
-        nc.vector.tensor_copy(
-            out=wg32[:, 512:768].rearrange("p (r u) -> p r u", u=2),
-            in_=wb1[:, 0:256].rearrange("p (u r) -> p r u", u=2),
-        )
-
-        def setup_small():
+        def setup_weights():
+            wb0 = new_bank("wb0")
+            word_transposes(wb0, 0, w_sb[:, 0, :])
+            word_transposes(wb0, 1, w_sb[:, 1, :])
+            wb1 = new_bank("wb1")
+            word_transposes(wb1, 0, w_sb[:, 2, :])
+            wg32 = w_grp[:].bitcast(F32)
+            nc.vector.tensor_copy(
+                out=wg32[:, 0:512].rearrange("p (a r u) -> p a r u", a=2, u=2),
+                in_=wb0[:].rearrange("p (a u r) -> p a r u", a=2, u=2),
+            )
+            nc.vector.tensor_copy(
+                out=wg32[:, 512:768].rearrange("p (r u) -> p r u", u=2),
+                in_=wb1[:, 0:256].rearrange("p (u r) -> p r u", u=2),
+            )
             for s in range(NS):
                 nc.vector.quantize_mx(
                     out=w_codes[:, s * P : (s + 1) * P].bitcast(FP8X4),
                     scales=w_scl[:, s * P : (s + 1) * P],
                     in_=w_grp[:, s * K : (s + 1) * K],
                 )
+
+        def setup_columns():
             nc.vector.tensor_copy(out=small_f[:], in_=small_bf[:])
             sb = new_bank("sb")
             nc.tensor.transpose(out=sb[:, 0:P], in_=small_f[:], identity=ident[:])
             nc.vector.tensor_copy(out=cols[:], in_=sb[:, 0:9])
+
+        def setup_bias():
             bb = new_bank("bb")
             for s in range(NS):
                 spread(bb, cols[:, s : s + 1], s)
             nc.vector.tensor_copy(out=bias_b[:], in_=bb[:, 0:OC])
 
-        for k in range(NR + 3):
-            if k + 2 < NR:
-                load(k + 2)
-            if 0 <= k - 2 < NR:
-                p2(k - 2)
-            if 0 <= k - 3 < NR:
-                flip(k - 3, "fl")
-            if k < NR:
-                t_in(k)
-            if k == 0:
-                setup_small()
-            if 0 <= k - 1 < NR:
-                quant(k - 1)
-            if 0 <= k - 3 < NR:
-                bn(k - 3)
-            if 0 <= k - 1 < NR:
-                mx(k - 1)
-                p1(k - 1)
-            if 0 <= k - 2 < NR:
-                norm(k - 2)
-                p3(k - 2)
+        for n in range(NS * NR + 15):
+            v = valid(n + 2 * NS)
+            if v is not None:
+                load(v[0], v[1], 1)
+            v = valid(n - 12)
+            if v is not None:
+                bn(v[0], v[1])
+            v = valid(n - 3)
+            if v is not None:
+                p1(v[0], v[1])
+            w = valid(n - 6)
+            if w is not None and w[1] < 2:
+                p2(w[0], 2 * w[1])
+            v = valid(n)
+            if v is not None:
+                t_in(v[0], v[1])
+            if n == 0:
+                setup_weights()
+            if n == 1:
+                setup_columns()
+            if n == 2:
+                setup_bias()
+            v = valid(n - 1)
+            if v is not None:
+                quant(v[0], v[1])
+            if w is not None and w[1] < 2:
+                p2(w[0], 2 * w[1] + 1)
+            if w is not None and w[1] == 1:
+                root(w[0])
+            if w is not None and w[1] == 2:
+                norm(w[0])
+                p3(w[0], 0, False)
+                p3(w[0], 3, True)
+            v = valid(n - 9)
+            if v is not None and v[1] < 2:
+                p3(v[0], v[1] + 1, False)
+            v = valid(n - 11)
+            if v is not None:
+                flip(v[0], v[1], "fl", False)
+            v = valid(n - 2)
+            if v is not None:
+                mx(v[0], v[1])
 
-        s_groups = list(S_GROUPS)
         v_groups = [g for g in range(NR) if g not in S_GROUPS]
-        flip(s_groups[0], "f1")
+        items = [(g, s) for g in S_GROUPS for s in range(NS)]
+        n_i = len(items)
+        flip(items[0][0], items[0][1], "f1", False)
+        flip(items[1][0], items[1][1], "f1", False)
         for s in range(NS):
             nc.vector.bn_aggr(out=mv[:, s, :], in_=stats[:, s, :, :].rearrange("p g x -> p (g x)"))
         nc.vector.tensor_scalar_add(out=veps[:], in0=mv[:, :, 1], scalar1=1e-5)
@@ -275,35 +322,28 @@ def tile_batchedgraphsagemean1_pb_t_kernel(
         o_t = {}
         obk = {}
 
-        def affine(g):
-            for s in range(NS):
-                ot = work.tile([P, TG * P], F32, name="ot%d" % s, tag="ot%d" % s)
-                o_t[(g, s)] = ot
-                nc.scalar.activation(
-                    out=ot[:],
-                    in_=fbk[(g, s)][:],
-                    func=ACT.Identity,
-                    scale=gain[:, s : s + 1],
-                    bias=shift[:, s : s + 1],
+        def affine(i):
+            g, s = items[i]
+            ot = tailp.tile([P, TG * P], F32, name="ot", tag="ot")
+            o_t[i] = ot
+            nc.scalar.activation(
+                out=ot[:], in_=fbk[(g, s)][:], func=ACT.Identity, scale=gain[:, s : s + 1], bias=shift[:, s : s + 1]
+            )
+
+        def flip_back(i):
+            bank = new_bank("f2")
+            obk[i] = bank
+            for j in range(TG):
+                nc.tensor.transpose(
+                    out=bank[:, j * P : (j + 1) * P], in_=o_t[i][:, j * P : (j + 1) * P], identity=ident[:]
                 )
 
-        def flip_back(g):
-            for s in range(NS):
-                bank = new_bank("f2")
-                obk[(g, s)] = bank
-                for j in range(TG):
-                    nc.tensor.transpose(
-                        out=bank[:, j * P : (j + 1) * P],
-                        in_=o_t[(g, s)][:, j * P : (j + 1) * P],
-                        identity=ident[:],
-                    )
-
-        def copy_back(g):
-            for s in range(NS):
-                nc.scalar.copy(
-                    out=res[:, g * TG : (g + 1) * TG, s * P : (s + 1) * P],
-                    in_=obk[(g, s)][:].rearrange("p (j c) -> p j c", j=TG),
-                )
+        def copy_back(i):
+            g, s = items[i]
+            nc.scalar.copy(
+                out=res[:, g * TG : (g + 1) * TG, s * P : (s + 1) * P],
+                in_=obk[i][:].rearrange("p (j c) -> p j c", j=TG),
+            )
 
         def store(g):
             nc.sync.dma_start(out=out_v[:, g * TG : (g + 1) * TG, :], in_=res[:, g * TG : (g + 1) * TG, :])
@@ -314,27 +354,28 @@ def tile_batchedgraphsagemean1_pb_t_kernel(
                 out=rs, in0=rs, in1=bank[:, 0:OC].unsqueeze(1).to_broadcast([P, TG, OC]), op=op
             )
 
-        n_s = len(s_groups)
-        n_v = len(v_groups)
-
         def v_pair(first):
-            pair = v_groups[first : first + 2]
-            for g in pair:
+            for g in v_groups[first : first + 2]:
                 v_scale(g, a_bank, ALU.mult)
-            for g in pair:
+            for g in v_groups[first : first + 2]:
                 v_scale(g, b_bank, ALU.add)
-                store(g)
 
-        affine(s_groups[0])
-        for i in range(n_s):
-            if i + 1 < n_s:
-                flip(s_groups[i + 1], "f1")
-            flip_back(s_groups[i])
-            if i % 2 == 0 and i < n_v:
-                v_pair(i)
-            if i + 1 < n_s:
-                affine(s_groups[i + 1])
-            copy_back(s_groups[i])
-            store(s_groups[i])
-        for i in range((n_s + 1) // 2 * 2, n_v, 2):
-            v_pair(i)
+        affine(0)
+        for i in range(n_i):
+            if i % 6 == 0:
+                v_pair(i // 3)
+            if i + 2 < n_i:
+                flip(items[i + 2][0], items[i + 2][1], "f1", TAIL_WARM)
+            flip_back(i)
+            if i + 1 < n_i:
+                affine(i + 1)
+            copy_back(i)
+            if items[i][1] == NS - 1:
+                store(items[i][0])
+            if i % 6 == 5:
+                for g in v_groups[i // 6 * 2 : i // 6 * 2 + 2]:
+                    store(g)
+        for first in range(n_i // 3, len(v_groups), 2):
+            v_pair(first)
+            for g in v_groups[first : first + 2]:
+                store(g)

@@ -24,8 +24,8 @@ FLOPS = 2 * ROWS * K * OC
 PIN = True
 XS_BUFS = 3
 V_EVAC_ROUNDS = 1
-DUMMY = True
-TAIL_WARM = True
+DUMMY = False
+TAIL_WARM = False
 S_GROUPS = (0, 2, 4, 6, 8, 10, 12, 14)
 
 

@@ -23,10 +23,11 @@ FLOPS = 2 * ROWS * K * OC
 
 PIN = True
 XS_BUFS = 3
-V_EVAC_ROUNDS = 1
+V_EVAC_ROUNDS = 0
 DUMMY = False
 TAIL_WARM = False
-S_GROUPS = (0, 2, 4, 6, 8, 10, 12, 14)
+S_GROUPS = (0, 2, 4, 6, 8, 10)
+G_GROUPS = (1, 3, 5)
 
 
 def tile_batchedgraphsagemean1_pb_t_kernel(
@@ -69,6 +70,8 @@ def tile_batchedgraphsagemean1_pb_t_kernel(
         gain = const.tile([P, NS], F32, name="gain")
         mgain = const.tile([P, NS], F32, name="mgain")
         shift = const.tile([P, NS], F32, name="shift")
+        a_row = const.tile([P, OC], F32, name="a_row")
+        b_row = const.tile([P, OC], F32, name="b_row")
 
         xs = {}
         grp = {}
@@ -291,7 +294,7 @@ def tile_batchedgraphsagemean1_pb_t_kernel(
                 p3(w[0], 3, True)
             v = valid(n - 9)
             if v is not None and v[1] < 2:
-                p3(v[0], v[1] + 1, False)
+                p3(v[0], v[1] + 1, v[1] == 1 and v[0] % 2 == 1)
             v = valid(n - 11)
             if v is not None:
                 flip(v[0], v[1], "fl", False)
@@ -299,7 +302,7 @@ def tile_batchedgraphsagemean1_pb_t_kernel(
             if v is not None:
                 mx(v[0], v[1])
 
-        v_groups = [g for g in range(NR) if g not in S_GROUPS]
+        v_groups = [g for g in range(NR) if g not in S_GROUPS and g not in G_GROUPS]
         items = [(g, s) for g in S_GROUPS for s in range(NS)]
         n_i = len(items)
         flip(items[0][0], items[0][1], "f1", False)
@@ -348,22 +351,38 @@ def tile_batchedgraphsagemean1_pb_t_kernel(
         def store(g):
             nc.sync.dma_start(out=out_v[:, g * TG : (g + 1) * TG, :], in_=res[:, g * TG : (g + 1) * TG, :])
 
-        def v_scale(g, bank, op):
-            rs = res[:, g * TG : (g + 1) * TG, :]
+        def v_scale(t0, n_t, bank, op):
+            rs = res[:, t0 : t0 + n_t, :]
             nc.vector.tensor_tensor(
-                out=rs, in0=rs, in1=bank[:, 0:OC].unsqueeze(1).to_broadcast([P, TG, OC]), op=op
+                out=rs, in0=rs, in1=bank[:, 0:OC].unsqueeze(1).to_broadcast([P, n_t, OC]), op=op
             )
+
+        def g_scale(g, row, op):
+            rs = res[:, g * TG : (g + 1) * TG, :]
+            nc.gpsimd.tensor_tensor(out=rs, in0=rs, in1=row[:].unsqueeze(1).to_broadcast([P, TG, OC]), op=op)
+
+        g0 = v_groups[0]
+        for j in range(TG):
+            v_scale(g0 * TG + j, 1, a_bank, ALU.mult)
+        nc.vector.tensor_copy(out=a_row[:], in_=a_bank[:, 0:OC])
+        for j in range(TG):
+            v_scale(g0 * TG + j, 1, b_bank, ALU.add)
+            nc.sync.dma_start(out=out_v[:, g0 * TG + j : g0 * TG + j + 1, :], in_=res[:, g0 * TG + j : g0 * TG + j + 1, :])
+        nc.vector.tensor_copy(out=b_row[:], in_=b_bank[:, 0:OC])
+        for g in G_GROUPS:
+            g_scale(g, a_row, ALU.mult)
+            g_scale(g, b_row, ALU.add)
 
         def v_pair(first):
             for g in v_groups[first : first + 2]:
-                v_scale(g, a_bank, ALU.mult)
+                v_scale(g * TG, TG, a_bank, ALU.mult)
             for g in v_groups[first : first + 2]:
-                v_scale(g, b_bank, ALU.add)
+                v_scale(g * TG, TG, b_bank, ALU.add)
 
         affine(0)
         for i in range(n_i):
             if i % 6 == 0:
-                v_pair(i // 3)
+                v_pair(1 + i // 3)
             if i + 2 < n_i:
                 flip(items[i + 2][0], items[i + 2][1], "f1", TAIL_WARM)
             flip_back(i)
@@ -373,9 +392,6 @@ def tile_batchedgraphsagemean1_pb_t_kernel(
             if items[i][1] == NS - 1:
                 store(items[i][0])
             if i % 6 == 5:
-                for g in v_groups[i // 6 * 2 : i // 6 * 2 + 2]:
+                for g in v_groups[1 + i // 6 * 2 : 3 + i // 6 * 2]:
                     store(g)
-        for first in range(n_i // 3, len(v_groups), 2):
-            v_pair(first)
-            for g in v_groups[first : first + 2]:
-                store(g)
+                store(G_GROUPS[i // 6])

@@ -21,8 +21,9 @@ TG = 4
 NR = NT // TG
 FLOPS = 2 * ROWS * K * OC
 
-PIN = True
+PIN = False
 XS_BUFS = 3
+PIN_END = True
 V_EVAC_ROUNDS = 0
 DUMMY = False
 TAIL_WARM = False
@@ -60,12 +61,9 @@ def tile_batchedgraphsagemean1_pb_t_kernel(
         w_scl = const.tile([P, NS * P], U8, name="w_scl", align_bytes=64)
         n2 = const.tile([P, NT], F32, name="n2")
         nrm = const.tile([P, NT], F32, name="nrm")
-        nrmc = const.tile([P, NT], F32, name="nrmc")
         invn = const.tile([P, NT], F32, name="invn")
         stats = const.tile([P, NS, NR, 6], F32, name="stats")
         mv = const.tile([P, NS, 2], F32, name="mv")
-        veps = const.tile([P, NS], F32, name="veps")
-        sdev = const.tile([P, NS], F32, name="sdev")
         rstd = const.tile([P, NS], F32, name="rstd")
         gain = const.tile([P, NS], F32, name="gain")
         mgain = const.tile([P, NS], F32, name="mgain")
@@ -162,12 +160,12 @@ def tile_batchedgraphsagemean1_pb_t_kernel(
             nc.scalar.activation(out=junk[:], in_=res[:, t, :], func=ACT.Square, accum_out=n2[:, t : t + 1])
 
         def root(g):
-            nc.scalar.sqrt(out=nrm[:, g * TG : (g + 1) * TG], in_=n2[:, g * TG : (g + 1) * TG])
+            sl = slice(g * TG, (g + 1) * TG)
+            nc.scalar.activation(out=nrm[:, sl], in_=n2[:, sl], func=ACT.Abs_reciprocal_sqrt)
 
         def norm(g):
             sl = slice(g * TG, (g + 1) * TG)
-            nc.vector.tensor_scalar_max(out=nrmc[:, sl], in0=nrm[:, sl], scalar1=1e-12)
-            nc.vector.reciprocal(out=invn[:, sl], in_=nrmc[:, sl])
+            nc.vector.tensor_scalar_min(out=invn[:, sl], in0=nrm[:, sl], scalar1=1e12)
 
         def p3(g, j, on_scalar):
             t = g * TG + j
@@ -302,6 +300,8 @@ def tile_batchedgraphsagemean1_pb_t_kernel(
             if v is not None:
                 mx(v[0], v[1])
 
+        if PIN_END:
+            ctx.enter_context(tc.manual_schedule())
         v_groups = [g for g in range(NR) if g not in S_GROUPS and g not in G_GROUPS]
         items = [(g, s) for g in S_GROUPS for s in range(NS)]
         n_i = len(items)
@@ -309,9 +309,7 @@ def tile_batchedgraphsagemean1_pb_t_kernel(
         flip(items[1][0], items[1][1], "f1", False)
         for s in range(NS):
             nc.vector.bn_aggr(out=mv[:, s, :], in_=stats[:, s, :, :].rearrange("p g x -> p (g x)"))
-        nc.vector.tensor_scalar_add(out=veps[:], in0=mv[:, :, 1], scalar1=1e-5)
-        nc.scalar.sqrt(out=sdev[:], in_=veps[:])
-        nc.vector.reciprocal(out=rstd[:], in_=sdev[:])
+        nc.scalar.activation(out=rstd[:], in_=mv[:, :, 1], func=ACT.Abs_reciprocal_sqrt, bias=1e-5)
         nc.vector.tensor_mul(out=gain[:], in0=cols[:, 3:6], in1=rstd[:])
         nc.vector.tensor_mul(out=mgain[:], in0=mv[:, :, 0], in1=gain[:])
         nc.vector.tensor_sub(out=shift[:], in0=cols[:, 6:9], in1=mgain[:])

@@ -51,8 +51,7 @@ def tile_batchedgraphsagemean1_pb_t_kernel(
 
         res = const.tile([P, NT, OC], F32, name="res")
         ident = const.tile([P, P], F32, name="ident")
-        small_bf = const.tile([P, P], BF16, name="small_bf")
-        small_f = const.tile([P, P], F32, name="small_f")
+        cols_bf = const.tile([P, 5, 16], BF16, name="cols_bf")
         cols = const.tile([P, 9], F32, name="cols")
         bias_b = const.tile([P, OC], F32, name="bias_b")
         w_sb = const.tile([P, NS, K], BF16, name="w_sb")
@@ -209,15 +208,21 @@ def tile_batchedgraphsagemean1_pb_t_kernel(
             g, s = divmod(n, NS)
             return (g, s) if 0 <= n and g < NR else None
 
-        nc.vector.memset(small_bf[:], 0.0)
         make_identity(nc, ident[:])
+        with nc.allow_non_contiguous_dma(reason="nine short vectors, one element to a partition"):
+            for s in range(NS):
+                nc.scalar.dma_start(out=cols_bf[:, s, 0:1], in_=biases[s].rearrange("(c o) -> c o", o=1))
+            nc.scalar.dma_start(
+                out=cols_bf[:, 3, 0:6].rearrange("p (s o) -> p s o", o=2)[:, :, 0:1],
+                in_=bn_gamma.rearrange("(s c o) -> c s o", s=NS, o=1),
+            )
+            nc.scalar.dma_start(
+                out=cols_bf[:, 4, 0:6].rearrange("p (s o) -> p s o", o=2)[:, :, 0:1],
+                in_=bn_beta.rearrange("(s c o) -> c s o", s=NS, o=1),
+            )
         load(0, 0, 2)
         for s in range(NS):
             nc.sync.dma_start(out=w_sb[:, s, :], in_=weights[s])
-        for s in range(NS):
-            nc.scalar.dma_start(out=small_bf[s : s + 1, :], in_=biases[s].unsqueeze(0))
-        nc.scalar.dma_start(out=small_bf[3:6, :], in_=bn_gamma.rearrange("(s c) -> s c", s=NS))
-        nc.scalar.dma_start(out=small_bf[6:9, :], in_=bn_beta.rearrange("(s c) -> s c", s=NS))
         load(0, 1, 1)
         load(0, 2, 1)
         for s in range(NS):
@@ -246,10 +251,10 @@ def tile_batchedgraphsagemean1_pb_t_kernel(
                 )
 
         def setup_columns():
-            nc.vector.tensor_copy(out=small_f[:], in_=small_bf[:])
-            sb = new_bank("sb")
-            nc.tensor.transpose(out=sb[:, 0:P], in_=small_f[:], identity=ident[:])
-            nc.vector.tensor_copy(out=cols[:], in_=sb[:, 0:9])
+            nc.vector.tensor_copy(out=cols[:, 0:3].unsqueeze(2), in_=cols_bf[:, 0:3, 0:1])
+            nc.vector.tensor_copy(
+                out=cols[:, 3:9].rearrange("p (v s) -> p v s", v=2), in_=cols_bf[:, 3:5, 0:6:2]
+            )
 
         def setup_bias():
             bb = new_bank("bb")

@@ -351,8 +351,8 @@ def tile_batchedgraphsagemean1_pb_t_kernel(
                 in_=obk[i][:].rearrange("p (j c) -> p j c", j=TG),
             )
 
-        def store(g):
-            nc.sync.dma_start(out=out_v[:, g * TG : (g + 1) * TG, :], in_=res[:, g * TG : (g + 1) * TG, :])
+        def store(t0, n_t):
+            nc.sync.dma_start(out=out_v[:, t0 : t0 + n_t, :], in_=res[:, t0 : t0 + n_t, :])
 
         def v_scale(t0, n_t, bank, op):
             rs = res[:, t0 : t0 + n_t, :]
@@ -360,32 +360,33 @@ def tile_batchedgraphsagemean1_pb_t_kernel(
                 out=rs, in0=rs, in1=bank[:, 0:OC].unsqueeze(1).to_broadcast([P, n_t, OC]), op=op
             )
 
-        def g_scale(g, row, op):
-            rs = res[:, g * TG : (g + 1) * TG, :]
-            nc.gpsimd.tensor_tensor(out=rs, in0=rs, in1=row[:].unsqueeze(1).to_broadcast([P, TG, OC]), op=op)
+        def g_piece(t0, n_t):
+            rs = res[:, t0 : t0 + n_t, :]
+            for row, op in ((a_row, ALU.mult), (b_row, ALU.add)):
+                nc.gpsimd.tensor_tensor(out=rs, in0=rs, in1=row[:].unsqueeze(1).to_broadcast([P, n_t, OC]), op=op)
+            store(t0, n_t)
 
-        g0 = v_groups[0]
-        for j in range(TG):
-            v_scale(g0 * TG + j, 1, a_bank, ALU.mult)
+        def v_group(g):
+            for h in range(2):
+                v_scale(g * TG + 2 * h, 2, a_bank, ALU.mult)
+            for h in range(2):
+                v_scale(g * TG + 2 * h, 2, b_bank, ALU.add)
+            store(g * TG, TG)
+
+        t0 = v_groups[0] * TG
+        v_scale(t0, 1, a_bank, ALU.mult)
+        v_scale(t0 + 1, 1, a_bank, ALU.mult)
+        v_scale(t0, 1, b_bank, ALU.add)
+        store(t0, 1)
+        v_scale(t0 + 1, 1, b_bank, ALU.add)
+        store(t0 + 1, 1)
         nc.vector.tensor_copy(out=a_row[:], in_=a_bank[:, 0:OC])
-        for j in range(TG):
-            v_scale(g0 * TG + j, 1, b_bank, ALU.add)
-            nc.sync.dma_start(out=out_v[:, g0 * TG + j : g0 * TG + j + 1, :], in_=res[:, g0 * TG + j : g0 * TG + j + 1, :])
+        v_scale(t0 + 2, 2, a_bank, ALU.mult)
         nc.vector.tensor_copy(out=b_row[:], in_=b_bank[:, 0:OC])
-        for g in G_GROUPS:
-            g_scale(g, a_row, ALU.mult)
-            g_scale(g, b_row, ALU.add)
 
-        def v_pair(first):
-            for g in v_groups[first : first + 2]:
-                v_scale(g * TG, TG, a_bank, ALU.mult)
-            for g in v_groups[first : first + 2]:
-                v_scale(g * TG, TG, b_bank, ALU.add)
-
+        g_after = {0: (G_GROUPS[0] * TG, 2), 1: (G_GROUPS[0] * TG + 2, 2), 3: (G_GROUPS[1] * TG, TG), 5: (G_GROUPS[2] * TG, TG)}
         affine(0)
         for i in range(n_i):
-            if i % 6 == 0:
-                v_pair(1 + i // 3)
             if i + 2 < n_i:
                 flip(items[i + 2][0], items[i + 2][1], "f1", TAIL_WARM)
             flip_back(i)
@@ -393,8 +394,14 @@ def tile_batchedgraphsagemean1_pb_t_kernel(
                 affine(i + 1)
             copy_back(i)
             if items[i][1] == NS - 1:
-                store(items[i][0])
-            if i % 6 == 5:
-                for g in v_groups[1 + i // 6 * 2 : 3 + i // 6 * 2]:
-                    store(g)
-                store(G_GROUPS[i // 6])
+                k = i // NS
+                store(items[i][0] * TG, TG)
+                if k == 0:
+                    v_scale(t0 + 2, 2, b_bank, ALU.add)
+                    store(t0 + 2, 2)
+                else:
+                    v_group(v_groups[k])
+                if k == n_i // NS - 1:
+                    v_group(v_groups[k + 1])
+                if k in g_after:
+                    g_piece(g_after[k][0], g_after[k][1])

@@ -96,7 +96,7 @@ def tile_batchedgraphsagemean1_pb_t_kernel(
                     out=t[:, i * w : (i + 1) * w, :], in_=feats[s][:, g * TG + i * w : g * TG + (i + 1) * w, :]
                 )
 
-        def t_in(g, s):
+        def t_in(g, s, between):
             gt = work.tile([P, TG * K], BF16, name="grp%d" % s, tag="grp%d" % s, align_bytes=64)
             grp[(g, s)] = gt
             g32 = gt[:].bitcast(F32)
@@ -110,6 +110,8 @@ def tile_batchedgraphsagemean1_pb_t_kernel(
                     nc.vector.tensor_copy(out=dst, in_=src)
                 else:
                     nc.scalar.copy(out=dst, in_=src)
+                if h == 0 and between is not None:
+                    root(between)
 
         def quant(g, s):
             ct = work.tile([P, TG * P], U32, name="codes%d" % s, tag="codes%d" % s, align_bytes=64)
@@ -276,8 +278,13 @@ def tile_batchedgraphsagemean1_pb_t_kernel(
             if w is not None and w[1] < 2:
                 p2(w[0], 2 * w[1])
             v = valid(n)
+            late_root = w[0] if w is not None and w[1] == 2 else None
             if v is not None:
-                t_in(v[0], v[1])
+                t_in(v[0], v[1], late_root)
+            elif late_root is not None:
+                root(late_root)
+            if late_root is not None:
+                norm(late_root)
             if n == 0:
                 setup_weights()
             if n == 1:
@@ -289,10 +296,7 @@ def tile_batchedgraphsagemean1_pb_t_kernel(
                 quant(v[0], v[1])
             if w is not None and w[1] < 2:
                 p2(w[0], 2 * w[1] + 1)
-            if w is not None and w[1] == 1:
-                root(w[0])
             if w is not None and w[1] == 2:
-                norm(w[0])
                 p3(w[0], 0, False)
                 p3(w[0], 3, True)
             v = valid(n - 9)

@@ -264,50 +264,51 @@ def tile_batchedgraphsagemean1_pb_t_kernel(
                 spread(bb, cols[:, s : s + 1], s)
             nc.vector.tensor_copy(out=bias_b[:], in_=bb[:, 0:OC])
 
-        for n in range(NS * NR + 15):
-            v = valid(n + 2 * NS)
-            if v is not None:
-                load(v[0], v[1], 1)
-            v = valid(n - 12)
-            if v is not None:
-                bn(v[0], v[1])
-            v = valid(n - 3)
-            if v is not None:
-                p1(v[0], v[1])
-            w = valid(n - 6)
-            if w is not None and w[1] < 2:
-                p2(w[0], 2 * w[1])
-            v = valid(n)
-            late_root = w[0] if w is not None and w[1] == 2 else None
-            if v is not None:
-                t_in(v[0], v[1], late_root)
-            elif late_root is not None:
-                root(late_root)
-            if late_root is not None:
-                norm(late_root)
-            if n == 0:
-                setup_weights()
-            if n == 1:
-                setup_columns()
-            if n == 2:
-                setup_bias()
-            v = valid(n - 1)
-            if v is not None:
-                quant(v[0], v[1])
-            if w is not None and w[1] < 2:
-                p2(w[0], 2 * w[1] + 1)
-            if w is not None and w[1] == 2:
-                p3(w[0], 0, False)
-                p3(w[0], 3, True)
-            v = valid(n - 9)
-            if v is not None and v[1] < 2:
-                p3(v[0], v[1] + 1, v[1] == 1 and v[0] % 2 == 1)
-            v = valid(n - 11)
-            if v is not None:
-                flip(v[0], v[1], "fl", False)
-            v = valid(n - 2)
-            if v is not None:
-                mx(v[0], v[1])
+        with tc.manual_schedule(engines={mybir.EngineType.PE}):
+            for n in range(NS * NR + 15):
+                v = valid(n + 2 * NS)
+                if v is not None:
+                    load(v[0], v[1], 1)
+                v = valid(n - 12)
+                if v is not None:
+                    bn(v[0], v[1])
+                v = valid(n - 3)
+                if v is not None:
+                    p1(v[0], v[1])
+                w = valid(n - 6)
+                if w is not None and w[1] < 2:
+                    p2(w[0], 2 * w[1])
+                v = valid(n)
+                late_root = w[0] if w is not None and w[1] == 2 else None
+                if v is not None:
+                    t_in(v[0], v[1], late_root)
+                elif late_root is not None:
+                    root(late_root)
+                if late_root is not None:
+                    norm(late_root)
+                if n == 0:
+                    setup_weights()
+                if n == 1:
+                    setup_columns()
+                if n == 2:
+                    setup_bias()
+                v = valid(n - 1)
+                if v is not None:
+                    quant(v[0], v[1])
+                if w is not None and w[1] < 2:
+                    p2(w[0], 2 * w[1] + 1)
+                if w is not None and w[1] == 2:
+                    p3(w[0], 0, False)
+                    p3(w[0], 3, True)
+                v = valid(n - 9)
+                if v is not None and v[1] < 2:
+                    p3(v[0], v[1] + 1, v[1] == 1 and v[0] % 2 == 1)
+                v = valid(n - 11)
+                if v is not None:
+                    flip(v[0], v[1], "fl", False)
+                v = valid(n - 2)
+                if v is not None:
+                    mx(v[0], v[1])
 
         if PIN_END:
             ctx.enter_context(tc.manual_schedule())

@@ -66,6 +66,7 @@ def tile_batchedgraphsagemean1_pb_t_kernel(
         rstd = const.tile([P, NS], F32, name="rstd")
         gain = const.tile([P, NS], F32, name="gain")
         mgain = const.tile([P, NS], F32, name="mgain")
+        mgam = const.tile([P, NS], F32, name="mgam")
         shift = const.tile([P, NS], F32, name="shift")
         a_row = const.tile([P, OC], F32, name="a_row")
         b_row = const.tile([P, OC], F32, name="b_row")
@@ -320,8 +321,9 @@ def tile_batchedgraphsagemean1_pb_t_kernel(
         for s in range(NS):
             nc.vector.bn_aggr(out=mv[:, s, :], in_=stats[:, s, :, :].rearrange("p g x -> p (g x)"))
         nc.scalar.activation(out=rstd[:], in_=mv[:, :, 1], func=ACT.Abs_reciprocal_sqrt, bias=1e-5)
+        nc.vector.tensor_mul(out=mgam[:], in0=mv[:, :, 0], in1=cols[:, 3:6])
+        nc.vector.tensor_mul(out=mgain[:], in0=mgam[:], in1=rstd[:])
         nc.vector.tensor_mul(out=gain[:], in0=cols[:, 3:6], in1=rstd[:])
-        nc.vector.tensor_mul(out=mgain[:], in0=mv[:, :, 0], in1=gain[:])
         nc.vector.tensor_sub(out=shift[:], in0=cols[:, 6:9], in1=mgain[:])
         a_bank = new_bank("a_bank")
         b_bank = new_bank("b_bank")
@@ -392,9 +394,9 @@ def tile_batchedgraphsagemean1_pb_t_kernel(
         g_after = {0: (G_GROUPS[0] * TG, 2), 1: (G_GROUPS[0] * TG + 2, 2), 3: (G_GROUPS[1] * TG, TG), 5: (G_GROUPS[2] * TG, TG)}
         affine(0)
         for i in range(n_i):
+            flip_back(i)
             if i + 2 < n_i:
                 flip(items[i + 2][0], items[i + 2][1], "f1", TAIL_WARM)
-            flip_back(i)
             if i + 1 < n_i:
                 affine(i + 1)
             copy_back(i)

@@ -67,6 +67,7 @@ def tile_batchedgraphsagemean1_pb_t_kernel(
         gain = const.tile([P, NS], F32, name="gain")
         mgain = const.tile([P, NS], F32, name="mgain")
         mgam = const.tile([P, NS], F32, name="mgam")
+        one = const.tile([P, 2], F32, name="one")
         shift = const.tile([P, NS], F32, name="shift")
         a_row = const.tile([P, OC], F32, name="a_row")
         b_row = const.tile([P, OC], F32, name="b_row")
@@ -211,6 +212,8 @@ def tile_batchedgraphsagemean1_pb_t_kernel(
             g, s = divmod(n, NS)
             return (g, s) if 0 <= n and g < NR else None
 
+        nc.vector.memset(one[:, 0:1], 1.0)
+        nc.scalar.activation(out=one[:, 1:2], in_=one[:, 0:1], func=ACT.Abs_reciprocal_sqrt)
         make_identity(nc, ident[:])
         with nc.allow_non_contiguous_dma(reason="nine short vectors, one element to a partition"):
             for s in range(NS):

@@ -306,7 +306,7 @@ def tile_batchedgraphsagemean1_pb_t_kernel(
                     p3(w[0], 3, True)
                 v = valid(n - 9)
                 if v is not None and v[1] < 2:
-                    p3(v[0], v[1] + 1, v[1] == 1 and v[0] % 2 == 1)
+                    p3(v[0], v[1] + 1, False)
                 v = valid(n - 11)
                 if v is not None:
                     flip(v[0], v[1], "fl", False)

from contextlib import ExitStack

import concourse.mybir as mybir
from concourse.masks import make_identity

F32 = mybir.dt.float32
BF16 = mybir.dt.bfloat16
U8 = mybir.dt.uint8
U32 = mybir.dt.uint32
FP8X4 = mybir.dt.float8_e4m3fn_x4
ALU = mybir.AluOpType
ACT = mybir.ActivationFunctionType

P = 128
ROWS = 8192
K = 512
NS = 3
OC = NS * P
NT = ROWS // P
TG = 4
NR = NT // TG
FLOPS = 2 * ROWS * K * OC

PIN = False
XS_BUFS = 3
PIN_END = True
V_EVAC_ROUNDS = 0
DUMMY = False
TAIL_WARM = False
S_GROUPS = (0, 2, 4, 6, 8, 10)
G_GROUPS = (1, 3, 5)


def tile_batchedgraphsagemean1_pb_t_kernel(
    tc, x, nb, mu, Wx_w, Wx_b, Wn_w, Wn_b, Wr_w, Wr_b, bn_gamma, bn_beta, out
):
    nc = tc.nc
    feats = [a.flatten_outer_dims().rearrange("(p t) k -> p t k", t=NT) for a in (x, nb, mu)]
    out_v = out.flatten_outer_dims().rearrange("(p t) c -> p t c", t=NT)
    weights = (Wx_w, Wn_w, Wr_w)
    biases = (Wx_b, Wn_b, Wr_b)

    with ExitStack() as ctx:
        if PIN:
            ctx.enter_context(tc.manual_schedule())
        const = ctx.enter_context(tc.tile_pool(name="const", bufs=1))
        loads = ctx.enter_context(tc.tile_pool(name="loads", bufs=XS_BUFS))
        work = ctx.enter_context(tc.tile_pool(name="work", bufs=2))
        tailp = ctx.enter_context(tc.tile_pool(name="tailp", bufs=3))
        psum = ctx.enter_context(tc.psum_pool(name="psum", bufs=8))

        res = const.tile([P, NT, OC], F32, name="res")
        ident = const.tile([P, P], F32, name="ident")
        cols_bf = const.tile([P, 5, 16], BF16, name="cols_bf")
        cols = const.tile([P, 9], F32, name="cols")
        bias_b = const.tile([P, OC], F32, name="bias_b")
        w_sb = const.tile([P, NS, K], BF16, name="w_sb")
        w_grp = const.tile([P, NS * K], BF16, name="w_grp", align_bytes=64)
        w_codes = const.tile([P, NS * P], U32, name="w_codes", align_bytes=64)
        w_scl = const.tile([P, NS * P], U8, name="w_scl", align_bytes=64)
        n2 = const.tile([P, NT], F32, name="n2")
        nrm = const.tile([P, NT], F32, name="nrm")
        invn = const.tile([P, NT], F32, name="invn")
        stats = const.tile([P, NS, NR, 6], F32, name="stats")
        mv = const.tile([P, NS, 2], F32, name="mv")
        rstd = const.tile([P, NS], F32, name="rstd")
        gain = const.tile([P, NS], F32, name="gain")
        mgain = const.tile([P, NS], F32, name="mgain")
        mgam = const.tile([P, NS], F32, name="mgam")
        one = const.tile([P, 2], F32, name="one")
        shift = const.tile([P, NS], F32, name="shift")
        a_row = const.tile([P, OC], F32, name="a_row")
        b_row = const.tile([P, OC], F32, name="b_row")

        xs = {}
        grp = {}
        codes = {}
        scl = {}
        mxb = {}
        fbk = {}

        def new_bank(label):
            bank = psum.tile([P, 512], F32, name=label, tag="bank")
            return bank

        def word_transposes(bank, a, src_bf):
            src = src_bf.bitcast(F32)
            for u in range(2):
                c = (2 * a + u) * P
                nc.tensor.transpose(out=bank[:, c : c + P], in_=src[:, u * P : (u + 1) * P], identity=ident[:])

        def load(g, s, parts):
            t = loads.tile([P, TG, K], BF16, name="xs%d" % s, tag="xs%d" % s)
            xs[(g, s)] = t
            w = TG // parts
            for i in range(parts):
                nc.sync.dma_start(
                    out=t[:, i * w : (i + 1) * w, :], in_=feats[s][:, g * TG + i * w : g * TG + (i + 1) * w, :]
                )

        def t_in(g, s, between):
            gt = work.tile([P, TG * K], BF16, name="grp%d" % s, tag="grp%d" % s, align_bytes=64)
            grp[(g, s)] = gt
            g32 = gt[:].bitcast(F32)
            for h in range(TG // 2):
                bank = new_bank("xt")
                for a in range(2):
                    word_transposes(bank, a, xs[(g, s)][:, 2 * h + a, :])
                dst = g32[:, h * 512 : (h + 1) * 512].rearrange("p (a r u) -> p a r u", a=2, u=2)
                src = bank[:].rearrange("p (a u r) -> p a r u", a=2, u=2)
                if g < V_EVAC_ROUNDS and h == 1:
                    nc.vector.tensor_copy(out=dst, in_=src)
                else:
                    nc.scalar.copy(out=dst, in_=src)
                if h == 0 and between is not None:
                    root(between)

        def quant(g, s):
            ct = work.tile([P, TG * P], U32, name="codes%d" % s, tag="codes%d" % s, align_bytes=64)
            st = work.tile([P, TG * P], U8, name="scl%d" % s, tag="scl%d" % s, align_bytes=64)
            codes[(g, s)] = ct
            scl[(g, s)] = st
            nc.vector.quantize_mx(out=ct[:].bitcast(FP8X4), scales=st[:], in_=grp[(g, s)][:])

        def clock_pass(bank, key):
            nc.tensor.matmul_mx(
                out=bank[:],
                lhsT=codes[key][:, 0:P].bitcast(FP8X4),
                lhsT_scale=scl[key][:, 0:P],
                rhs=codes[key][:].bitcast(FP8X4),
                rhs_scale=scl[key][:],
                start=True,
                stop=True,
            )

        def mx(g, s):
            bank = new_bank("mx")
            mxb[(g, s)] = bank
            if DUMMY:
                clock_pass(bank, (g, s))
            for j in range(TG):
                nc.tensor.matmul_mx(
                    out=bank[:, j * P : (j + 1) * P],
                    lhsT=codes[(g, s)][:, j * P : (j + 1) * P].bitcast(FP8X4),
                    lhsT_scale=scl[(g, s)][:, j * P : (j + 1) * P],
                    rhs=w_codes[:, s * P : (s + 1) * P].bitcast(FP8X4),
                    rhs_scale=w_scl[:, s * P : (s + 1) * P],
                    start=True,
                    stop=True,
                )

        def p1(g, s):
            nc.vector.tensor_tensor(
                out=res[:, g * TG : (g + 1) * TG, s * P : (s + 1) * P],
                in0=mxb[(g, s)][:].rearrange("p (j c) -> p j c", j=TG),
                in1=bias_b[:, s * P : (s + 1) * P].unsqueeze(1).to_broadcast([P, TG, P]),
                op=ALU.add,
            )

        def p2(g, j):
            t = g * TG + j
            junk = work.tile([P, OC], F32, name="junk", tag="junk")
            nc.scalar.activation(out=junk[:], in_=res[:, t, :], func=ACT.Square, accum_out=n2[:, t : t + 1])

        def root(g):
            sl = slice(g * TG, (g + 1) * TG)
            nc.scalar.activation(out=nrm[:, sl], in_=n2[:, sl], func=ACT.Abs_reciprocal_sqrt)

        def norm(g):
            sl = slice(g * TG, (g + 1) * TG)
            nc.vector.tensor_scalar_min(out=invn[:, sl], in0=nrm[:, sl], scalar1=1e12)

        def p3(g, j, on_scalar):
            t = g * TG + j
            if on_scalar:
                nc.scalar.activation(out=res[:, t, :], in_=res[:, t, :], func=ACT.Relu, scale=invn[:, t : t + 1])
            else:
                nc.vector.tensor_scalar(
                    out=res[:, t, :],
                    in0=res[:, t, :],
                    scalar1=invn[:, t : t + 1],
                    scalar2=0.0,
                    op0=ALU.mult,
                    op1=ALU.max,
                )

        def flip(g, s, label, warm):
            bank = new_bank(label)
            fbk[(g, s)] = bank
            if warm:
                clock_pass(bank, (NR - 1, NS - 1))
            for j in range(TG):
                nc.tensor.transpose(
                    out=bank[:, j * P : (j + 1) * P],
                    in_=res[:, g * TG + j, s * P : (s + 1) * P],
                    identity=ident[:],
                )

        def bn(g, s):
            nc.vector.bn_stats(out=stats[:, s, g, :], in_=fbk[(g, s)][:])

        def spread(bank, vec, m):
            nc.tensor.matmul(
                out=bank[:, m * P : (m + 1) * P],
                lhsT=vec.to_broadcast([P, P]),
                rhs=ident[:],
                start=True,
                stop=True,
            )

        def valid(n):
            g, s = divmod(n, NS)
            return (g, s) if 0 <= n and g < NR else None

        nc.vector.memset(one[:, 0:1], 1.0)
        nc.scalar.activation(out=one[:, 1:2], in_=one[:, 0:1], func=ACT.Abs_reciprocal_sqrt)
        make_identity(nc, ident[:])
        with nc.allow_non_contiguous_dma(reason="nine short vectors, one element to a partition"):
            for s in range(NS):
                nc.scalar.dma_start(out=cols_bf[:, s, 0:1], in_=biases[s].rearrange("(c o) -> c o", o=1))
            nc.scalar.dma_start(
                out=cols_bf[:, 3, 0:6].rearrange("p (s o) -> p s o", o=2)[:, :, 0:1],
                in_=bn_gamma.rearrange("(s c o) -> c s o", s=NS, o=1),
            )
            nc.scalar.dma_start(
                out=cols_bf[:, 4, 0:6].rearrange("p (s o) -> p s o", o=2)[:, :, 0:1],
                in_=bn_beta.rearrange("(s c o) -> c s o", s=NS, o=1),
            )
        load(0, 0, 2)
        for s in range(NS):
            nc.sync.dma_start(out=w_sb[:, s, :], in_=weights[s])
        load(0, 1, 1)
        load(0, 2, 1)
        for s in range(NS):
            load(1, s, 1)

        def setup_weights():
            wb0 = new_bank("wb0")
            word_transposes(wb0, 0, w_sb[:, 0, :])
            word_transposes(wb0, 1, w_sb[:, 1, :])
            wb1 = new_bank("wb1")
            word_transposes(wb1, 0, w_sb[:, 2, :])
            wg32 = w_grp[:].bitcast(F32)
            nc.vector.tensor_copy(
                out=wg32[:, 0:512].rearrange("p (a r u) -> p a r u", a=2, u=2),
                in_=wb0[:].rearrange("p (a u r) -> p a r u", a=2, u=2),
            )
            nc.vector.tensor_copy(
                out=wg32[:, 512:768].rearrange("p (r u) -> p r u", u=2),
                in_=wb1[:, 0:256].rearrange("p (u r) -> p r u", u=2),
            )
            for s in range(NS):
                nc.vector.quantize_mx(
                    out=w_codes[:, s * P : (s + 1) * P].bitcast(FP8X4),
                    scales=w_scl[:, s * P : (s + 1) * P],
                    in_=w_grp[:, s * K : (s + 1) * K],
                )

        def setup_columns():
            nc.vector.tensor_copy(out=cols[:, 0:3].unsqueeze(2), in_=cols_bf[:, 0:3, 0:1])
            nc.vector.tensor_copy(
                out=cols[:, 3:9].rearrange("p (v s) -> p v s", v=2), in_=cols_bf[:, 3:5, 0:6:2]
            )

        def setup_bias():
            bb = new_bank("bb")
            for s in range(NS):
                spread(bb, cols[:, s : s + 1], s)
            nc.vector.tensor_copy(out=bias_b[:], in_=bb[:, 0:OC])

        with tc.manual_schedule(engines={mybir.EngineType.PE}):
            for n in range(NS * NR + 15):
                v = valid(n + 2 * NS)
                if v is not None:
                    load(v[0], v[1], 1)
                v = valid(n - 12)
                if v is not None:
                    bn(v[0], v[1])
                v = valid(n - 3)
                if v is not None:
                    p1(v[0], v[1])
                w = valid(n - 6)
                if w is not None and w[1] < 2:
                    p2(w[0], 2 * w[1])
                v = valid(n)
                late_root = w[0] if w is not None and w[1] == 2 else None
                if v is not None:
                    t_in(v[0], v[1], late_root)
                elif late_root is not None:
                    root(late_root)
                if late_root is not None:
                    norm(late_root)
                if n == 0:
                    setup_weights()
                if n == 1:
                    setup_columns()
                if n == 2:
                    setup_bias()
                v = valid(n - 1)
                if v is not None:
                    quant(v[0], v[1])
                if w is not None and w[1] < 2:
                    p2(w[0], 2 * w[1] + 1)
                if w is not None and w[1] == 2:
                    p3(w[0], 0, False)
                    p3(w[0], 3, True)
                v = valid(n - 9)
                if v is not None and v[1] < 2:
                    p3(v[0], v[1] + 1, False)
                v = valid(n - 11)
                if v is not None:
                    flip(v[0], v[1], "fl", False)
                v = valid(n - 2)
                if v is not None:
                    mx(v[0], v[1])

        if PIN_END:
            ctx.enter_context(tc.manual_schedule())
        v_groups = [g for g in range(NR) if g not in S_GROUPS and g not in G_GROUPS]
        items = [(g, s) for g in S_GROUPS for s in range(NS)]
        n_i = len(items)
        flip(items[0][0], items[0][1], "f1", False)
        flip(items[1][0], items[1][1], "f1", False)
        for s in range(NS):
            nc.vector.bn_aggr(out=mv[:, s, :], in_=stats[:, s, :, :].rearrange("p g x -> p (g x)"))
        nc.scalar.activation(out=rstd[:], in_=mv[:, :, 1], func=ACT.Abs_reciprocal_sqrt, bias=1e-5)
        nc.vector.tensor_mul(out=mgam[:], in0=mv[:, :, 0], in1=cols[:, 3:6])
        nc.vector.tensor_mul(out=mgain[:], in0=mgam[:], in1=rstd[:])
        nc.vector.tensor_mul(out=gain[:], in0=cols[:, 3:6], in1=rstd[:])
        nc.vector.tensor_sub(out=shift[:], in0=cols[:, 6:9], in1=mgain[:])
        a_bank = new_bank("a_bank")
        b_bank = new_bank("b_bank")
        for s in range(NS):
            spread(a_bank, gain[:, s : s + 1], s)
        for s in range(NS):
            spread(b_bank, shift[:, s : s + 1], s)

        o_t = {}
        obk = {}

        def affine(i):
            g, s = items[i]
            ot = tailp.tile([P, TG * P], F32, name="ot", tag="ot")
            o_t[i] = ot
            nc.scalar.activation(
                out=ot[:], in_=fbk[(g, s)][:], func=ACT.Identity, scale=gain[:, s : s + 1], bias=shift[:, s : s + 1]
            )

        def flip_back(i):
            bank = new_bank("f2")
            obk[i] = bank
            for j in range(TG):
                nc.tensor.transpose(
                    out=bank[:, j * P : (j + 1) * P], in_=o_t[i][:, j * P : (j + 1) * P], identity=ident[:]
                )

        def copy_back(i):
            g, s = items[i]
            nc.scalar.copy(
                out=res[:, g * TG : (g + 1) * TG, s * P : (s + 1) * P],
                in_=obk[i][:].rearrange("p (j c) -> p j c", j=TG),
            )

        def store(t0, n_t):
            nc.sync.dma_start(out=out_v[:, t0 : t0 + n_t, :], in_=res[:, t0 : t0 + n_t, :])

        def v_scale(t0, n_t, bank, op):
            rs = res[:, t0 : t0 + n_t, :]
            nc.vector.tensor_tensor(
                out=rs, in0=rs, in1=bank[:, 0:OC].unsqueeze(1).to_broadcast([P, n_t, OC]), op=op
            )

        def g_piece(t0, n_t):
            rs = res[:, t0 : t0 + n_t, :]
            for row, op in ((a_row, ALU.mult), (b_row, ALU.add)):
                nc.gpsimd.tensor_tensor(out=rs, in0=rs, in1=row[:].unsqueeze(1).to_broadcast([P, n_t, OC]), op=op)
            store(t0, n_t)

        def v_group(g):
            for h in range(2):
                v_scale(g * TG + 2 * h, 2, a_bank, ALU.mult)
            for h in range(2):
                v_scale(g * TG + 2 * h, 2, b_bank, ALU.add)
            store(g * TG, TG)

        t0 = v_groups[0] * TG
        v_scale(t0, 1, a_bank, ALU.mult)
        v_scale(t0 + 1, 1, a_bank, ALU.mult)
        v_scale(t0, 1, b_bank, ALU.add)
        store(t0, 1)
        v_scale(t0 + 1, 1, b_bank, ALU.add)
        store(t0 + 1, 1)
        nc.vector.tensor_copy(out=a_row[:], in_=a_bank[:, 0:OC])
        v_scale(t0 + 2, 2, a_bank, ALU.mult)
        nc.vector.tensor_copy(out=b_row[:], in_=b_bank[:, 0:OC])

        g_after = {0: (G_GROUPS[0] * TG, 2), 1: (G_GROUPS[0] * TG + 2, 2), 3: (G_GROUPS[1] * TG, TG), 5: (G_GROUPS[2] * TG, TG)}
        affine(0)
        for i in range(n_i):
            flip_back(i)
            if i + 2 < n_i:
                flip(items[i + 2][0], items[i + 2][1], "f1", TAIL_WARM)
            if i + 1 < n_i:
                affine(i + 1)
            copy_back(i)
            if items[i][1] == NS - 1:
                k = i // NS
                store(items[i][0] * TG, TG)
                if k == 0:
                    v_scale(t0 + 2, 2, b_bank, ALU.add)
                    store(t0 + 2, 2)
                else:
                    v_group(v_groups[k])
                if k == n_i // NS - 1:
                    v_group(v_groups[k + 1])
                if k in g_after:
                    g_piece(g_after[k][0], g_after[k][1])
